import numpy as np
import ml_dtypes


def mxq(x, axis, fmt="e4m3"):
    dtype, down = {"e4m3": (ml_dtypes.float8_e4m3fn, 7), "e5m2": (ml_dtypes.float8_e5m2, 14)}[fmt]
    v = np.moveaxis(np.asarray(x, np.float32).astype(ml_dtypes.bfloat16).astype(np.float64), axis, -1)
    blocks = v.reshape(v.shape[:-1] + (-1, 32))
    amax = np.abs(blocks).max(-1, keepdims=True)
    byte = np.maximum(np.where(amax > 0, np.frexp(amax)[1] - 1 + 127, 0) - down, 1)
    scale = np.exp2(byte - 127.0)
    codes = (blocks / scale).astype(np.float32).astype(dtype).astype(np.float64)
    return np.moveaxis((codes * scale).reshape(v.shape), -1, axis)


WIDE = False


def mx_kscale(k):
    if not WIDE:
        return np.ones(k)
    levels = np.array([10, -10, 5, -5, 0])
    a = np.random.permutation(np.resize(levels, k // 512 * 4)).reshape(k // 512, 4)
    idx = np.arange(k)
    return np.exp2(a[idx // 512, idx % 128 // 32])


BF16 = ml_dtypes.bfloat16


def bf(x):
    return np.asarray(x, np.float32).astype(BF16)


def f64(x):
    return np.asarray(x).astype(np.float64)


B, N, IN_DIM, OUT_DIM, K = 8, 512, 512, 128, 3
EPS = 1e-6
SIG = 2.0


def laplacian(adj):
    d = adj.sum(axis=2)
    r = (d + EPS) ** -0.5
    return np.eye(N)[None] - r[:, :, None] * adj * r[:, None, :]


def setup_inputs():
    s, u = mx_kscale(N), mx_kscale(IN_DIM)
    sn = s / s.max()
    return {"x": bf(np.random.standard_normal((B, N, IN_DIM)) * sn[:, None] * u),
            "tx1": bf(np.random.standard_normal((B, N, IN_DIM)) * sn[:, None] * u),
            "adj": bf(np.exp(SIG * np.random.standard_normal((B, N, N)) - SIG * SIG / 2.0) / N * (s * s)[:, None]),
            "W": bf(np.random.standard_normal((K, IN_DIM, OUT_DIM)) / np.sqrt(IN_DIM) / u[:, None]),
            "b": bf(np.random.standard_normal((K, OUT_DIM)) * 0.3)}


def reference(x, tx1, adj, W, b):
    x, tx1, b = f64(x), f64(tx1), f64(b)
    Wq = mxq(f64(W), 1, "e4m3")
    L = laplacian(f64(adj))
    out = (mxq(x, 2, "e4m3") @ Wq[0]) + b[0] + (mxq(tx1, 2, "e4m3") @ Wq[1]) + b[1]
    tx2 = 2.0 * (mxq(L, 2, "e4m3") @ mxq(tx1, 1, "e4m3")) - x
    out = out + (mxq(tx2, 2, "e4m3") @ Wq[2]) + b[2]
    return np.maximum(out, 0.0)

@@ -1,0 +1,278 @@
+from contextlib import ExitStack
+
+import concourse.mybir as mybir
+from concourse.masks import make_identity
+
+F32 = mybir.dt.float32
+BF16 = mybir.dt.bfloat16
+U32 = mybir.dt.uint32
+U8 = mybir.dt.uint8
+FP8X4 = mybir.dt.float8_e4m3fn_x4
+ALU = mybir.AluOpType
+ACT = mybir.ActivationFunctionType
+
+P = 128
+PACK = 4
+GRAPHS = 8
+NODES = 512
+FEATS = 512
+OUTS = 128
+ORDERS = 3
+TILES = NODES // P
+HALF = FEATS // 2
+EPS = 1e-6
+
+FLOPS = 2 * GRAPHS * (NODES * NODES * FEATS + ORDERS * NODES * FEATS * OUTS)
+
+
+def tile_cheblayer_pb_kernel(tc, x, tx1, adj, W, b, out):
+    nc = tc.nc
+    with ExitStack() as ctx:
+        const = ctx.enter_context(tc.tile_pool(name="const", bufs=1))
+        inputs = ctx.enter_context(tc.tile_pool(name="inputs", bufs=GRAPHS))
+        small = ctx.enter_context(tc.tile_pool(name="small", bufs=3))
+        work = ctx.enter_context(tc.tile_pool(name="work", bufs=2))
+        turned = ctx.enter_context(tc.psum_pool(name="turned", bufs=3))
+        product = ctx.enter_context(tc.psum_pool(name="product", bufs=TILES))
+        result = ctx.enter_context(tc.psum_pool(name="result", bufs=1))
+        ctx.enter_context(tc.manual_schedule())
+
+        x_nat, tx1_nat, adj_nat = {}, {}, {}
+        root, inv, neg_inv, rows = {}, {}, {}, {}
+        x_grp, lap_q, tx1_node_q, x_q, tx1_feat_q, tx2_q = {}, {}, {}, {}, {}, {}
+        tx1_feat_grp, tx1_node_grp, lap_grp, tx2_grp, prod, out_by_feat = {}, {}, {}, {}, {}, {}
+
+        eps = const.tile([P, 1], F32)
+        nc.vector.memset(eps[:], EPS)
+        warm = const.tile([P, 1], F32)
+        nc.scalar.activation(out=warm[:], in_=eps[:], func=ACT.Sqrt)
+        ident = const.tile([P, P], F32)
+        make_identity(nc, ident[:])
+        scrap = const.tile([P, TILES, NODES], BF16)
+
+        def load_graph(g):
+            adj_t = inputs.tile([P, TILES, NODES], BF16, tag="adj_nat")
+            nc.sync.dma_start(out=adj_t[:], in_=adj[g].rearrange("(a p) j -> p a j", p=P))
+            tx1_t = inputs.tile([P, TILES, FEATS], BF16, tag="tx1_nat")
+            nc.sync.dma_start(out=tx1_t[:], in_=tx1[g].rearrange("(a p) f -> p a f", p=P))
+            x_t = inputs.tile([P, TILES, FEATS], BF16, tag="x_nat")
+            nc.sync.dma_start(out=x_t[:], in_=x[g].rearrange("(a p) f -> p a f", p=P))
+            adj_nat[g], tx1_nat[g], x_nat[g] = adj_t, tx1_t, x_t
+
+        load_graph(0)
+        w_nat = const.tile([P, ORDERS * 2, 2 * OUTS], BF16)
+        nc.sync.dma_start(
+            out=w_nat[:], in_=W.rearrange("k (u p e) o -> p (k u) (e o)", u=2, e=2)
+        )
+        b_all = const.tile([P, ORDERS * OUTS], BF16)
+        nc.sync.dma_start(out=b_all[:], in_=b.rearrange("k o -> (k o)").partition_broadcast(P))
+        for g in range(1, GRAPHS):
+            load_graph(g)
+
+        def quantise(grouped, tag):
+            columns = grouped.shape[1]
+            codes = work.tile([P, columns], U32, tag=tag + "_codes", name=tag + "_codes", align_bytes=64)
+            scales = work.tile([P, columns], U8, tag=tag + "_scales", name=tag + "_scales", align_bytes=64)
+            nc.vector.quantize_mx(
+                out=codes[:].bitcast(FP8X4),
+                scales=scales[:],
+                in_=grouped[:].rearrange("p c t -> p (c t)"),
+            )
+            return codes, scales
+
+        def mx(out_ap, stationary, s_cols, moving, m_cols, start, stop):
+            nc.tensor.matmul_mx(
+                out=out_ap,
+                lhsT=stationary[0][:, s_cols].bitcast(FP8X4),
+                lhsT_scale=stationary[1][:, s_cols],
+                rhs=moving[0][:, m_cols].bitcast(FP8X4),
+                rhs_scale=moving[1][:, m_cols],
+                start=start,
+                stop=stop,
+            )
+
+        def tile_cols(a):
+            return slice(a * P, (a + 1) * P)
+
+        w_grp = const.tile([P, ORDERS, OUTS, PACK], BF16, align_bytes=64)
+        w_codes = const.tile([P, ORDERS * OUTS], U32, align_bytes=64)
+        w_scales = const.tile([P, ORDERS * OUTS], U8, align_bytes=64)
+        bias_sum = const.tile([P, OUTS], F32)
+        bias_col = const.tile([P, 1], F32)
+
+        def prepare_weights():
+            for k in range(ORDERS):
+                nc.vector.tensor_copy(
+                    out=w_grp[:, k].rearrange("p o (u e) -> p o u e", u=2),
+                    in_=w_nat[:, 2 * k : 2 * k + 2, :].rearrange("p u (e o) -> p o u e", e=2),
+                )
+            for k in range(ORDERS):
+                nc.vector.quantize_mx(
+                    out=w_codes[:, tile_cols(k)].bitcast(FP8X4),
+                    scales=w_scales[:, tile_cols(k)],
+                    in_=w_grp[:, k].rearrange("p o t -> p (o t)"),
+                )
+            nc.vector.tensor_tensor(
+                out=bias_sum[:], in0=b_all[:, tile_cols(0)], in1=b_all[:, tile_cols(1)], op=ALU.add
+            )
+            nc.vector.tensor_tensor(
+                out=bias_sum[:], in0=bias_sum[:], in1=b_all[:, tile_cols(2)], op=ALU.add
+            )
+            bank = turned.tile([P, P], F32, tag="turned")
+            nc.tensor.transpose(bank[:], bias_sum[:], ident[:])
+            nc.vector.tensor_copy(out=bias_col[:], in_=bank[:, 0:1])
+
+        def degrees(g):
+            deg = small.tile([P, TILES], F32, tag="deg")
+            for a in range(TILES):
+                nc.scalar.activation(
+                    out=scrap[:, a, :], in_=adj_nat[g][:, a, :], func=ACT.Copy,
+                    accum_out=deg[:, a : a + 1],
+                )
+            root_t = small.tile([P, TILES], F32, tag="root")
+            nc.scalar.activation(out=root_t[:], in_=deg[:], func=ACT.Sqrt, bias=eps[:, 0:1])
+            root[g] = root_t
+
+        def inverse_roots(g):
+            inv_t = small.tile([P, TILES], F32, tag="inv")
+            nc.vector.reciprocal(out=inv_t[:], in_=root[g][:])
+            neg_t = small.tile([P, TILES], F32, tag="neg_inv")
+            nc.vector.tensor_scalar(
+                out=neg_t[:], in0=inv_t[:], scalar1=-1.0, scalar2=None, op0=ALU.mult
+            )
+            inv[g], neg_inv[g] = inv_t, neg_t
+
+        def scale_rows(g):
+            rows_t = work.tile([P, TILES, NODES], F32, tag="rows")
+            for a in range(TILES):
+                nc.gpsimd.tensor_scalar(
+                    out=rows_t[:, a, :], in0=adj_nat[g][:, a, :],
+                    scalar1=neg_inv[g][:, a : a + 1], scalar2=0.0, op0=ALU.mult, op1=ALU.add,
+                )
+            rows[g] = rows_t
+
+        def add_diagonal(g):
+            for a in range(TILES):
+                block = rows[g][:, a, tile_cols(a)]
+                nc.vector.scalar_tensor_tensor(
+                    out=block, in0=ident[:], scalar=root[g][:, a : a + 1], in1=block,
+                    op0=ALU.mult, op1=ALU.add,
+                )
+
+        def laplacian(g):
+            lap_t = work.tile([P, NODES, PACK], BF16, tag="lap_grp", align_bytes=64)
+            for a in range(TILES):
+                bank = turned.tile([P, PACK, P], F32, tag="turned")
+                for t in range(PACK):
+                    nc.tensor.transpose(bank[:, t, :], rows[g][:, a, tile_cols(t)], ident[:])
+                nc.vector.tensor_tensor(
+                    out=lap_t[:, tile_cols(a), :],
+                    in0=bank[:].rearrange("p t c -> p c t"),
+                    in1=inv[g][:].unsqueeze(1).to_broadcast([P, P, PACK]),
+                    op=ALU.mult,
+                )
+            lap_grp[g] = lap_t
+
+        def group_by_node(g):
+            grp = work.tile([P, FEATS, PACK], BF16, tag="tx1_node_grp", align_bytes=64)
+            src = tx1_nat[g][:].rearrange("p t (u m e) -> p u e m t", u=2, e=2)
+            dst = grp[:].rearrange("p (u e m) t -> p u e m t", u=2, e=2)
+            nc.scalar.copy(out=dst[:, 0], in_=src[:, 0])
+            nc.gpsimd.tensor_scalar(
+                out=dst[:, 1], in0=src[:, 1], scalar1=1.0, scalar2=0.0, op0=ALU.mult, op1=ALU.add
+            )
+            tx1_node_grp[g] = grp
+
+        def turn_features(nat, tag):
+            grp = work.tile([P, NODES, PACK], BF16, tag=tag, name=tag, align_bytes=64)
+            words_in = nat[:].bitcast(F32)
+            words_out = (
+                grp[:].rearrange("p i t -> p (i t)").bitcast(F32).rearrange("p (i u) -> p i u", u=2)
+            )
+            for h in range(2):
+                bank = turned.tile([P, 2, 2 * P], F32, tag="turned")
+                for u in range(2):
+                    for a2 in range(2):
+                        nc.tensor.transpose(
+                            bank[:, u, tile_cols(a2)], words_in[:, 2 * h + a2, tile_cols(u)], ident[:]
+                        )
+                nc.scalar.copy(
+                    out=words_out[:, 2 * P * h : 2 * P * (h + 1), :],
+                    in_=bank[:].rearrange("p u c -> p c u"),
+                )
+            return grp
+
+        def first_product(g):
+            prod[g] = []
+            for a in range(TILES):
+                bank = product.tile([P, PACK, P], F32, tag="product")
+                for v in range(PACK):
+                    mx(bank[:, v, :], tx1_node_q[g], tile_cols(v), lap_q[g], tile_cols(a), True, True)
+                prod[g].append(bank)
+
+        def second_order(g):
+            grp = work.tile([P, NODES, PACK], BF16, tag="tx2_grp", align_bytes=64)
+            for a in range(TILES):
+                nc.vector.scalar_tensor_tensor(
+                    out=grp[:, tile_cols(a), :],
+                    in0=prod[g][a][:].rearrange("p v c -> p c v"),
+                    scalar=2.0,
+                    in1=x_grp[g][:, tile_cols(a), :],
+                    op0=ALU.mult,
+                    op1=ALU.subtract,
+                )
+            tx2_grp[g] = grp
+
+        def output_product(g):
+            acc = result.tile([P, NODES], F32, tag="result")
+            terms = (x_q[g], tx1_feat_q[g], tx2_q[g])
+            for k in range(ORDERS):
+                mx(acc[:], (w_codes, w_scales), tile_cols(k), terms[k], slice(0, NODES),
+                   k == 0, k == ORDERS - 1)
+            by_feat = work.tile([P, NODES], F32, tag="out_by_feat")
+            nc.scalar.activation(out=by_feat[:], in_=acc[:], func=ACT.Relu, bias=bias_col[:, 0:1])
+            out_by_feat[g] = by_feat
+
+        def store_output(g):
+            bank = turned.tile([P, TILES, OUTS], F32, tag="turned")
+            for a in range(TILES):
+                nc.tensor.transpose(bank[:, a, :], out_by_feat[g][:, tile_cols(a)], ident[:])
+            by_node = work.tile([P, TILES, OUTS], F32, tag="out_by_node")
+            nc.scalar.copy(out=by_node[:], in_=bank[:])
+            nc.sync.dma_start(out=out[g].rearrange("(a p) o -> p a o", p=P), in_=by_node[:])
+
+        def live(g):
+            return 0 <= g < GRAPHS
+
+        for s in range(-2, GRAPHS + 1):
+            if live(s + 1):
+                group_by_node(s + 1)
+            if s == -1:
+                prepare_weights()
+            if live(s):
+                laplacian(s)
+            if live(s - 1):
+                output_product(s - 1)
+            if live(s):
+                lap_q[s] = quantise(lap_grp[s], "lap")
+                first_product(s)
+            if live(s - 1):
+                store_output(s - 1)
+            if live(s + 1):
+                x_grp[s + 1] = turn_features(x_nat[s + 1], "x_grp")
+                tx1_feat_grp[s + 1] = turn_features(tx1_nat[s + 1], "tx1_feat_grp")
+            if live(s + 2):
+                degrees(s + 2)
+            if live(s):
+                x_q[s] = quantise(x_grp[s], "x")
+            if live(s + 1):
+                inverse_roots(s + 1)
+                scale_rows(s + 1)
+            if live(s):
+                second_order(s)
+                tx1_feat_q[s] = quantise(tx1_feat_grp[s], "tx1_feat")
+            if live(s + 1):
+                tx1_node_q[s + 1] = quantise(tx1_node_grp[s + 1], "tx1_node")
+                add_diagonal(s + 1)
+            if live(s):
+                tx2_q[s] = quantise(tx2_grp[s], "tx2")

@@ -38,7 +38,7 @@ def tile_cheblayer_pb_kernel(tc, x, tx1, adj, W, b, out):
         ctx.enter_context(tc.manual_schedule())
 
         x_nat, tx1_nat, adj_nat = {}, {}, {}
-        root, inv, neg_inv, rows = {}, {}, {}, {}
+        root, inv, rows = {}, {}, {}
         x_grp, lap_q, tx1_node_q, x_q, tx1_feat_q, tx2_q = {}, {}, {}, {}, {}, {}
         tx1_feat_grp, tx1_node_grp, lap_grp, tx2_grp, prod, out_by_feat = {}, {}, {}, {}, {}, {}
 
@@ -52,7 +52,12 @@ def tile_cheblayer_pb_kernel(tc, x, tx1, adj, W, b, out):
 
         def load_graph(g):
             adj_t = inputs.tile([P, TILES, NODES], BF16, tag="adj_nat")
-            nc.sync.dma_start(out=adj_t[:], in_=adj[g].rearrange("(a p) j -> p a j", p=P))
+            adj_rows = adj[g].rearrange("(a p) j -> p a j", p=P)
+            if g == 0:
+                for a in range(TILES):
+                    nc.sync.dma_start(out=adj_t[:, a, :], in_=adj_rows[:, a, :])
+            else:
+                nc.sync.dma_start(out=adj_t[:], in_=adj_rows)
             tx1_t = inputs.tile([P, TILES, FEATS], BF16, tag="tx1_nat")
             nc.sync.dma_start(out=tx1_t[:], in_=tx1[g].rearrange("(a p) f -> p a f", p=P))
             x_t = inputs.tile([P, TILES, FEATS], BF16, tag="x_nat")
@@ -136,18 +141,14 @@ def tile_cheblayer_pb_kernel(tc, x, tx1, adj, W, b, out):
         def inverse_roots(g):
             inv_t = small.tile([P, TILES], F32, tag="inv")
             nc.vector.reciprocal(out=inv_t[:], in_=root[g][:])
-            neg_t = small.tile([P, TILES], F32, tag="neg_inv")
-            nc.vector.tensor_scalar(
-                out=neg_t[:], in0=inv_t[:], scalar1=-1.0, scalar2=None, op0=ALU.mult
-            )
-            inv[g], neg_inv[g] = inv_t, neg_t
+            inv[g] = inv_t
 
         def scale_rows(g):
             rows_t = work.tile([P, TILES, NODES], F32, tag="rows")
             for a in range(TILES):
-                nc.gpsimd.tensor_scalar(
+                nc.vector.tensor_scalar(
                     out=rows_t[:, a, :], in0=adj_nat[g][:, a, :],
-                    scalar1=neg_inv[g][:, a : a + 1], scalar2=0.0, op0=ALU.mult, op1=ALU.add,
+                    scalar1=inv[g][:, a : a + 1], scalar2=-1.0, op0=ALU.mult, op1=ALU.mult,
                 )
             rows[g] = rows_t
 
@@ -175,12 +176,10 @@ def tile_cheblayer_pb_kernel(tc, x, tx1, adj, W, b, out):
 
         def group_by_node(g):
             grp = work.tile([P, FEATS, PACK], BF16, tag="tx1_node_grp", align_bytes=64)
-            src = tx1_nat[g][:].rearrange("p t (u m e) -> p u e m t", u=2, e=2)
-            dst = grp[:].rearrange("p (u e m) t -> p u e m t", u=2, e=2)
-            nc.scalar.copy(out=dst[:, 0], in_=src[:, 0])
-            nc.gpsimd.tensor_scalar(
-                out=dst[:, 1], in0=src[:, 1], scalar1=1.0, scalar2=0.0, op0=ALU.mult, op1=ALU.add
-            )
+            src = tx1_nat[g][:].rearrange("p t (u m e) -> p u m e t", u=2, e=2)
+            dst = grp[:].rearrange("p (u e m) t -> p u m e t", u=2, e=2)
+            for u in range(2):
+                nc.scalar.copy(out=dst[:, u], in_=src[:, u])
             tx1_node_grp[g] = grp
 
         def turn_features(nat, tag):

@@ -32,15 +32,16 @@ def tile_cheblayer_pb_kernel(tc, x, tx1, adj, W, b, out):
         inputs = ctx.enter_context(tc.tile_pool(name="inputs", bufs=GRAPHS))
         small = ctx.enter_context(tc.tile_pool(name="small", bufs=3))
         work = ctx.enter_context(tc.tile_pool(name="work", bufs=2))
+        chain = ctx.enter_context(tc.psum_pool(name="chain", bufs=TILES))
         turned = ctx.enter_context(tc.psum_pool(name="turned", bufs=3))
-        product = ctx.enter_context(tc.psum_pool(name="product", bufs=TILES))
         result = ctx.enter_context(tc.psum_pool(name="result", bufs=1))
         ctx.enter_context(tc.manual_schedule())
 
         x_nat, tx1_nat, adj_nat = {}, {}, {}
         root, inv, rows = {}, {}, {}
         x_grp, lap_q, tx1_node_q, x_q, tx1_feat_q, tx2_q = {}, {}, {}, {}, {}, {}
-        tx1_feat_grp, tx1_node_grp, lap_grp, tx2_grp, prod, out_by_feat = {}, {}, {}, {}, {}, {}
+        tx1_feat_grp, tx1_node_grp, lap_grp, tx2_grp = {}, {}, {}, {}
+        rows_turned, prod, out_by_feat, out_turned = {}, {}, {}, {}
 
         eps = const.tile([P, 1], F32)
         nc.vector.memset(eps[:], EPS)
@@ -50,29 +51,32 @@ def tile_cheblayer_pb_kernel(tc, x, tx1, adj, W, b, out):
         make_identity(nc, ident[:])
         scrap = const.tile([P, TILES, NODES], BF16)
 
-        def load_graph(g):
+        def load_adjacency(g, pieces):
             adj_t = inputs.tile([P, TILES, NODES], BF16, tag="adj_nat")
             adj_rows = adj[g].rearrange("(a p) j -> p a j", p=P)
-            if g == 0:
-                for a in range(TILES):
-                    nc.sync.dma_start(out=adj_t[:, a, :], in_=adj_rows[:, a, :])
-            else:
-                nc.sync.dma_start(out=adj_t[:], in_=adj_rows)
+            step = TILES // pieces
+            for a in range(0, TILES, step):
+                nc.sync.dma_start(out=adj_t[:, a : a + step, :], in_=adj_rows[:, a : a + step, :])
+            adj_nat[g] = adj_t
+
+        def load_features(g):
             tx1_t = inputs.tile([P, TILES, FEATS], BF16, tag="tx1_nat")
             nc.sync.dma_start(out=tx1_t[:], in_=tx1[g].rearrange("(a p) f -> p a f", p=P))
             x_t = inputs.tile([P, TILES, FEATS], BF16, tag="x_nat")
             nc.sync.dma_start(out=x_t[:], in_=x[g].rearrange("(a p) f -> p a f", p=P))
-            adj_nat[g], tx1_nat[g], x_nat[g] = adj_t, tx1_t, x_t
+            tx1_nat[g], x_nat[g] = tx1_t, x_t
 
-        load_graph(0)
+        load_adjacency(0, pieces=TILES)
         w_nat = const.tile([P, ORDERS * 2, 2 * OUTS], BF16)
         nc.sync.dma_start(
             out=w_nat[:], in_=W.rearrange("k (u p e) o -> p (k u) (e o)", u=2, e=2)
         )
         b_all = const.tile([P, ORDERS * OUTS], BF16)
         nc.sync.dma_start(out=b_all[:], in_=b.rearrange("k o -> (k o)").partition_broadcast(P))
+        load_features(0)
         for g in range(1, GRAPHS):
-            load_graph(g)
+            load_adjacency(g, pieces=1)
+            load_features(g)
 
         def quantise(grouped, tag):
             columns = grouped.shape[1]
@@ -160,15 +164,18 @@ def tile_cheblayer_pb_kernel(tc, x, tx1, adj, W, b, out):
                     op0=ALU.mult, op1=ALU.add,
                 )
 
+        def turn_rows(g, a):
+            bank = chain.tile([P, PACK, P], F32, tag="chain")
+            for t in range(PACK):
+                nc.tensor.transpose(bank[:, t, :], rows[g][:, a, tile_cols(t)], ident[:])
+            rows_turned[g, a] = bank
+
         def laplacian(g):
             lap_t = work.tile([P, NODES, PACK], BF16, tag="lap_grp", align_bytes=64)
             for a in range(TILES):
-                bank = turned.tile([P, PACK, P], F32, tag="turned")
-                for t in range(PACK):
-                    nc.tensor.transpose(bank[:, t, :], rows[g][:, a, tile_cols(t)], ident[:])
                 nc.vector.tensor_tensor(
                     out=lap_t[:, tile_cols(a), :],
-                    in0=bank[:].rearrange("p t c -> p c t"),
+                    in0=rows_turned[g, a][:].rearrange("p t c -> p c t"),
                     in1=inv[g][:].unsqueeze(1).to_broadcast([P, P, PACK]),
                     op=ALU.mult,
                 )
@@ -202,25 +209,21 @@ def tile_cheblayer_pb_kernel(tc, x, tx1, adj, W, b, out):
             return grp
 
         def first_product(g):
-            prod[g] = []
             for a in range(TILES):
-                bank = product.tile([P, PACK, P], F32, tag="product")
+                bank = chain.tile([P, PACK, P], F32, tag="chain")
                 for v in range(PACK):
                     mx(bank[:, v, :], tx1_node_q[g], tile_cols(v), lap_q[g], tile_cols(a), True, True)
-                prod[g].append(bank)
+                prod[g, a] = bank
 
-        def second_order(g):
-            grp = work.tile([P, NODES, PACK], BF16, tag="tx2_grp", align_bytes=64)
-            for a in range(TILES):
-                nc.vector.scalar_tensor_tensor(
-                    out=grp[:, tile_cols(a), :],
-                    in0=prod[g][a][:].rearrange("p v c -> p c v"),
-                    scalar=2.0,
-                    in1=x_grp[g][:, tile_cols(a), :],
-                    op0=ALU.mult,
-                    op1=ALU.subtract,
-                )
-            tx2_grp[g] = grp
+        def second_order(g, a):
+            nc.vector.scalar_tensor_tensor(
+                out=tx2_grp[g][:, tile_cols(a), :],
+                in0=prod[g, a][:].rearrange("p v c -> p c v"),
+                scalar=2.0,
+                in1=x_grp[g][:, tile_cols(a), :],
+                op0=ALU.mult,
+                op1=ALU.subtract,
+            )
 
         def output_product(g):
             acc = result.tile([P, NODES], F32, tag="result")
@@ -232,46 +235,55 @@ def tile_cheblayer_pb_kernel(tc, x, tx1, adj, W, b, out):
             nc.scalar.activation(out=by_feat[:], in_=acc[:], func=ACT.Relu, bias=bias_col[:, 0:1])
             out_by_feat[g] = by_feat
 
-        def store_output(g):
+        def turn_output(g):
             bank = turned.tile([P, TILES, OUTS], F32, tag="turned")
             for a in range(TILES):
                 nc.tensor.transpose(bank[:, a, :], out_by_feat[g][:, tile_cols(a)], ident[:])
+            out_turned[g] = bank
+
+        def store_output(g):
             by_node = work.tile([P, TILES, OUTS], F32, tag="out_by_node")
-            nc.scalar.copy(out=by_node[:], in_=bank[:])
+            nc.scalar.copy(out=by_node[:], in_=out_turned[g][:])
             nc.sync.dma_start(out=out[g].rearrange("(a p) o -> p a o", p=P), in_=by_node[:])
 
         def live(g):
             return 0 <= g < GRAPHS
 
         for s in range(-2, GRAPHS + 1):
-            if live(s + 1):
-                group_by_node(s + 1)
             if s == -1:
                 prepare_weights()
-            if live(s):
-                laplacian(s)
             if live(s - 1):
                 output_product(s - 1)
             if live(s):
+                laplacian(s)
+            if live(s + 1):
+                x_grp[s + 1] = turn_features(x_nat[s + 1], "x_grp")
+            if live(s):
+                x_q[s] = quantise(x_grp[s], "x")
                 lap_q[s] = quantise(lap_grp[s], "lap")
                 first_product(s)
             if live(s - 1):
-                store_output(s - 1)
+                turn_output(s - 1)
             if live(s + 1):
-                x_grp[s + 1] = turn_features(x_nat[s + 1], "x_grp")
                 tx1_feat_grp[s + 1] = turn_features(tx1_nat[s + 1], "tx1_feat_grp")
+            if live(s - 1):
+                store_output(s - 1)
             if live(s + 2):
                 degrees(s + 2)
+                group_by_node(s + 2)
             if live(s):
-                x_q[s] = quantise(x_grp[s], "x")
+                tx1_feat_q[s] = quantise(tx1_feat_grp[s], "tx1_feat")
+                tx2_grp[s] = work.tile([P, NODES, PACK], BF16, tag="tx2_grp", name="tx2_grp", align_bytes=64)
             if live(s + 1):
                 inverse_roots(s + 1)
                 scale_rows(s + 1)
-            if live(s):
-                second_order(s)
-                tx1_feat_q[s] = quantise(tx1_feat_grp[s], "tx1_feat")
+                add_diagonal(s + 1)
+            for a in range(TILES):
+                if live(s):
+                    second_order(s, a)
+                if live(s + 1):
+                    turn_rows(s + 1, a)
             if live(s + 1):
                 tx1_node_q[s + 1] = quantise(tx1_node_grp[s + 1], "tx1_node")
-                add_diagonal(s + 1)
             if live(s):
                 tx2_q[s] = quantise(tx2_grp[s], "tx2")

@@ -19,7 +19,6 @@ FEATS = 512
 OUTS = 128
 ORDERS = 3
 TILES = NODES // P
-HALF = FEATS // 2
 EPS = 1e-6
 
 FLOPS = 2 * GRAPHS * (NODES * NODES * FEATS + ORDERS * NODES * FEATS * OUTS)
@@ -33,15 +32,14 @@ def tile_cheblayer_pb_kernel(tc, x, tx1, adj, W, b, out):
         small = ctx.enter_context(tc.tile_pool(name="small", bufs=3))
         work = ctx.enter_context(tc.tile_pool(name="work", bufs=2))
         chain = ctx.enter_context(tc.psum_pool(name="chain", bufs=TILES))
-        turned = ctx.enter_context(tc.psum_pool(name="turned", bufs=3))
-        result = ctx.enter_context(tc.psum_pool(name="result", bufs=1))
+        turned = ctx.enter_context(tc.psum_pool(name="turned", bufs=4))
         ctx.enter_context(tc.manual_schedule())
 
         x_nat, tx1_nat, adj_nat = {}, {}, {}
-        root, inv, rows = {}, {}, {}
+        deg, root, inv, rows = {}, {}, {}, {}
         x_grp, lap_q, tx1_node_q, x_q, tx1_feat_q, tx2_q = {}, {}, {}, {}, {}, {}
         tx1_feat_grp, tx1_node_grp, lap_grp, tx2_grp = {}, {}, {}, {}
-        rows_turned, prod, out_by_feat, out_turned = {}, {}, {}, {}
+        rows_turned, prod, out_by_feat, out_turned, out_by_node = {}, {}, {}, {}, {}
 
         eps = const.tile([P, 1], F32)
         nc.vector.memset(eps[:], EPS)
@@ -78,16 +76,22 @@ def tile_cheblayer_pb_kernel(tc, x, tx1, adj, W, b, out):
             load_adjacency(g, pieces=1)
             load_features(g)
 
-        def quantise(grouped, tag):
-            columns = grouped.shape[1]
-            codes = work.tile([P, columns], U32, tag=tag + "_codes", name=tag + "_codes", align_bytes=64)
-            scales = work.tile([P, columns], U8, tag=tag + "_scales", name=tag + "_scales", align_bytes=64)
-            nc.vector.quantize_mx(
-                out=codes[:].bitcast(FP8X4),
-                scales=scales[:],
-                in_=grouped[:].rearrange("p c t -> p (c t)"),
-            )
+        def mx_operand(tag):
+            codes = work.tile([P, NODES], U32, tag=tag + "_codes", name=tag + "_codes", align_bytes=64)
+            scales = work.tile([P, NODES], U8, tag=tag + "_scales", name=tag + "_scales", align_bytes=64)
             return codes, scales
+
+        def quantise_cols(grouped, operand, cols):
+            nc.vector.quantize_mx(
+                out=operand[0][:, cols].bitcast(FP8X4),
+                scales=operand[1][:, cols],
+                in_=grouped[:, cols, :].rearrange("p c t -> p (c t)"),
+            )
+
+        def quantise(grouped, tag):
+            operand = mx_operand(tag)
+            quantise_cols(grouped, operand, slice(0, NODES))
+            return operand
 
         def mx(out_ap, stationary, s_cols, moving, m_cols, start, stop):
             nc.tensor.matmul_mx(
@@ -102,6 +106,9 @@ def tile_cheblayer_pb_kernel(tc, x, tx1, adj, W, b, out):
 
         def tile_cols(a):
             return slice(a * P, (a + 1) * P)
+
+        def half_cols(h):
+            return slice(h * NODES // 2, (h + 1) * NODES // 2)
 
         w_grp = const.tile([P, ORDERS, OUTS, PACK], BF16, align_bytes=64)
         w_codes = const.tile([P, ORDERS * OUTS], U32, align_bytes=64)
@@ -132,14 +139,17 @@ def tile_cheblayer_pb_kernel(tc, x, tx1, adj, W, b, out):
             nc.vector.tensor_copy(out=bias_col[:], in_=bank[:, 0:1])
 
         def degrees(g):
-            deg = small.tile([P, TILES], F32, tag="deg")
+            deg_t = small.tile([P, TILES], F32, tag="deg")
             for a in range(TILES):
                 nc.scalar.activation(
                     out=scrap[:, a, :], in_=adj_nat[g][:, a, :], func=ACT.Copy,
-                    accum_out=deg[:, a : a + 1],
+                    accum_out=deg_t[:, a : a + 1],
                 )
+            deg[g] = deg_t
+
+        def roots(g):
             root_t = small.tile([P, TILES], F32, tag="root")
-            nc.scalar.activation(out=root_t[:], in_=deg[:], func=ACT.Sqrt, bias=eps[:, 0:1])
+            nc.scalar.activation(out=root_t[:], in_=deg[g][:], func=ACT.Sqrt, bias=eps[:, 0:1])
             root[g] = root_t
 
         def inverse_roots(g):
@@ -225,26 +235,32 @@ def tile_cheblayer_pb_kernel(tc, x, tx1, adj, W, b, out):
                 op1=ALU.subtract,
             )
 
-        def output_product(g):
-            acc = result.tile([P, NODES], F32, tag="result")
+        def output_product(g, h):
+            if h == 0:
+                out_by_feat[g] = work.tile([P, NODES], F32, tag="out_by_feat", name="out_by_feat")
+            acc = turned.tile([P, NODES // 2], F32, tag="turned")
             terms = (x_q[g], tx1_feat_q[g], tx2_q[g])
             for k in range(ORDERS):
-                mx(acc[:], (w_codes, w_scales), tile_cols(k), terms[k], slice(0, NODES),
+                mx(acc[:], (w_codes, w_scales), tile_cols(k), terms[k], half_cols(h),
                    k == 0, k == ORDERS - 1)
-            by_feat = work.tile([P, NODES], F32, tag="out_by_feat")
-            nc.scalar.activation(out=by_feat[:], in_=acc[:], func=ACT.Relu, bias=bias_col[:, 0:1])
-            out_by_feat[g] = by_feat
+            nc.scalar.activation(
+                out=out_by_feat[g][:, half_cols(h)], in_=acc[:], func=ACT.Relu, bias=bias_col[:, 0:1]
+            )
 
-        def turn_output(g):
-            bank = turned.tile([P, TILES, OUTS], F32, tag="turned")
-            for a in range(TILES):
-                nc.tensor.transpose(bank[:, a, :], out_by_feat[g][:, tile_cols(a)], ident[:])
-            out_turned[g] = bank
+        def turn_output(g, h):
+            bank = turned.tile([P, 2, OUTS], F32, tag="turned")
+            for a2 in range(2):
+                nc.tensor.transpose(bank[:, a2, :], out_by_feat[g][:, tile_cols(2 * h + a2)], ident[:])
+            out_turned[g, h] = bank
 
-        def store_output(g):
-            by_node = work.tile([P, TILES, OUTS], F32, tag="out_by_node")
-            nc.scalar.copy(out=by_node[:], in_=out_turned[g][:])
-            nc.sync.dma_start(out=out[g].rearrange("(a p) o -> p a o", p=P), in_=by_node[:])
+        def store_output(g, h):
+            if h == 0:
+                out_by_node[g] = work.tile([P, TILES, OUTS], F32, tag="out_by_node", name="out_by_node")
+            tiles = slice(2 * h, 2 * h + 2)
+            nc.scalar.copy(out=out_by_node[g][:, tiles, :], in_=out_turned[g, h][:])
+            nc.sync.dma_start(
+                out=out[g].rearrange("(a p) o -> p a o", p=P)[:, tiles, :], in_=out_by_node[g][:, tiles, :]
+            )
 
         def live(g):
             return 0 <= g < GRAPHS
@@ -253,29 +269,36 @@ def tile_cheblayer_pb_kernel(tc, x, tx1, adj, W, b, out):
             if s == -1:
                 prepare_weights()
             if live(s - 1):
-                output_product(s - 1)
+                output_product(s - 1, 0)
+                output_product(s - 1, 1)
             if live(s):
                 laplacian(s)
             if live(s + 1):
                 x_grp[s + 1] = turn_features(x_nat[s + 1], "x_grp")
             if live(s):
                 x_q[s] = quantise(x_grp[s], "x")
+            if live(s + 1):
+                inverse_roots(s + 1)
+            if live(s):
                 lap_q[s] = quantise(lap_grp[s], "lap")
                 first_product(s)
             if live(s - 1):
-                turn_output(s - 1)
+                turn_output(s - 1, 0)
+                turn_output(s - 1, 1)
             if live(s + 1):
                 tx1_feat_grp[s + 1] = turn_features(tx1_nat[s + 1], "tx1_feat_grp")
             if live(s - 1):
-                store_output(s - 1)
+                store_output(s - 1, 0)
+                store_output(s - 1, 1)
             if live(s + 2):
                 degrees(s + 2)
+                roots(s + 2)
                 group_by_node(s + 2)
             if live(s):
                 tx1_feat_q[s] = quantise(tx1_feat_grp[s], "tx1_feat")
                 tx2_grp[s] = work.tile([P, NODES, PACK], BF16, tag="tx2_grp", name="tx2_grp", align_bytes=64)
+                tx2_q[s] = mx_operand("tx2")
             if live(s + 1):
-                inverse_roots(s + 1)
                 scale_rows(s + 1)
                 add_diagonal(s + 1)
             for a in range(TILES):
@@ -283,7 +306,9 @@ def tile_cheblayer_pb_kernel(tc, x, tx1, adj, W, b, out):
                     second_order(s, a)
                 if live(s + 1):
                     turn_rows(s + 1, a)
+                if live(s) and a == TILES - 2:
+                    quantise_cols(tx2_grp[s], tx2_q[s], half_cols(0))
             if live(s + 1):
                 tx1_node_q[s + 1] = quantise(tx1_node_grp[s + 1], "tx1_node")
             if live(s):
-                tx2_q[s] = quantise(tx2_grp[s], "tx2")
+                quantise_cols(tx2_grp[s], tx2_q[s], half_cols(1))

@@ -20,6 +20,7 @@ OUTS = 128
 ORDERS = 3
 TILES = NODES // P
 EPS = 1e-6
+VECTOR_ROW_TILES = 3
 
 FLOPS = 2 * GRAPHS * (NODES * NODES * FEATS + ORDERS * NODES * FEATS * OUTS)
 
@@ -36,7 +37,7 @@ def tile_cheblayer_pb_kernel(tc, x, tx1, adj, W, b, out):
         ctx.enter_context(tc.manual_schedule())
 
         x_nat, tx1_nat, adj_nat = {}, {}, {}
-        deg, root, inv, rows = {}, {}, {}, {}
+        deg, root, neg_root, inv, rows = {}, {}, {}, {}, {}
         x_grp, lap_q, tx1_node_q, x_q, tx1_feat_q, tx2_q = {}, {}, {}, {}, {}, {}
         tx1_feat_grp, tx1_node_grp, lap_grp, tx2_grp = {}, {}, {}, {}
         rows_turned, prod, out_by_feat, out_turned, out_by_node = {}, {}, {}, {}, {}
@@ -47,6 +48,8 @@ def tile_cheblayer_pb_kernel(tc, x, tx1, adj, W, b, out):
         nc.scalar.activation(out=warm[:], in_=eps[:], func=ACT.Sqrt)
         ident = const.tile([P, P], F32)
         make_identity(nc, ident[:])
+        ident_bf = const.tile([P, P], BF16)
+        make_identity(nc, ident_bf[:])
         scrap = const.tile([P, TILES, NODES], BF16)
 
         def load_adjacency(g, pieces):
@@ -69,8 +72,9 @@ def tile_cheblayer_pb_kernel(tc, x, tx1, adj, W, b, out):
         nc.sync.dma_start(
             out=w_nat[:], in_=W.rearrange("k (u p e) o -> p (k u) (e o)", u=2, e=2)
         )
-        b_all = const.tile([P, ORDERS * OUTS], BF16)
-        nc.sync.dma_start(out=b_all[:], in_=b.rearrange("k o -> (k o)").partition_broadcast(P))
+        b_rows = const.tile([P, P], BF16)
+        nc.vector.memset(b_rows[:], 0.0)
+        nc.sync.dma_start(out=b_rows[0:ORDERS, :], in_=b)
         load_features(0)
         for g in range(1, GRAPHS):
             load_adjacency(g, pieces=1)
@@ -113,7 +117,6 @@ def tile_cheblayer_pb_kernel(tc, x, tx1, adj, W, b, out):
         w_grp = const.tile([P, ORDERS, OUTS, PACK], BF16, align_bytes=64)
         w_codes = const.tile([P, ORDERS * OUTS], U32, align_bytes=64)
         w_scales = const.tile([P, ORDERS * OUTS], U8, align_bytes=64)
-        bias_sum = const.tile([P, OUTS], F32)
         bias_col = const.tile([P, 1], F32)
 
         def prepare_weights():
@@ -128,15 +131,11 @@ def tile_cheblayer_pb_kernel(tc, x, tx1, adj, W, b, out):
                     scales=w_scales[:, tile_cols(k)],
                     in_=w_grp[:, k].rearrange("p o t -> p (o t)"),
                 )
-            nc.vector.tensor_tensor(
-                out=bias_sum[:], in0=b_all[:, tile_cols(0)], in1=b_all[:, tile_cols(1)], op=ALU.add
+            bank = turned.tile([P, P], BF16, tag="turned")
+            nc.tensor.transpose(bank[:], b_rows[:], ident_bf[:])
+            nc.vector.tensor_reduce(
+                out=bias_col[:], in_=bank[:, 0:ORDERS], axis=mybir.AxisListType.X, op=ALU.add
             )
-            nc.vector.tensor_tensor(
-                out=bias_sum[:], in0=bias_sum[:], in1=b_all[:, tile_cols(2)], op=ALU.add
-            )
-            bank = turned.tile([P, P], F32, tag="turned")
-            nc.tensor.transpose(bank[:], bias_sum[:], ident[:])
-            nc.vector.tensor_copy(out=bias_col[:], in_=bank[:, 0:1])
 
         def degrees(g):
             deg_t = small.tile([P, TILES], F32, tag="deg")
@@ -150,27 +149,35 @@ def tile_cheblayer_pb_kernel(tc, x, tx1, adj, W, b, out):
         def roots(g):
             root_t = small.tile([P, TILES], F32, tag="root")
             nc.scalar.activation(out=root_t[:], in_=deg[g][:], func=ACT.Sqrt, bias=eps[:, 0:1])
-            root[g] = root_t
+            neg_t = small.tile([P, TILES], F32, tag="neg_root")
+            nc.scalar.activation(out=neg_t[:], in_=root_t[:], func=ACT.Copy, scale=-1.0)
+            root[g], neg_root[g] = root_t, neg_t
 
         def inverse_roots(g):
             inv_t = small.tile([P, TILES], F32, tag="inv")
             nc.vector.reciprocal(out=inv_t[:], in_=root[g][:])
             inv[g] = inv_t
 
-        def scale_rows(g):
-            rows_t = work.tile([P, TILES, NODES], F32, tag="rows")
-            for a in range(TILES):
-                nc.vector.tensor_scalar(
-                    out=rows_t[:, a, :], in0=adj_nat[g][:, a, :],
-                    scalar1=inv[g][:, a : a + 1], scalar2=-1.0, op0=ALU.mult, op1=ALU.mult,
+        def scale_rows_on_scalar(g):
+            rows[g] = work.tile([P, TILES, NODES], F32, tag="rows", name="rows")
+            for a in range(VECTOR_ROW_TILES, TILES):
+                nc.scalar.activation(
+                    out=rows[g][:, a, :], in_=adj_nat[g][:, a, :], func=ACT.Copy,
+                    scale=inv[g][:, a : a + 1],
                 )
-            rows[g] = rows_t
 
-        def add_diagonal(g):
+        def scale_rows_on_vector(g):
+            for a in range(VECTOR_ROW_TILES):
+                nc.vector.tensor_scalar(
+                    out=rows[g][:, a, :], in0=adj_nat[g][:, a, :],
+                    scalar1=inv[g][:, a : a + 1], scalar2=None, op0=ALU.mult,
+                )
+
+        def subtract_diagonal(g):
             for a in range(TILES):
                 block = rows[g][:, a, tile_cols(a)]
                 nc.vector.scalar_tensor_tensor(
-                    out=block, in0=ident[:], scalar=root[g][:, a : a + 1], in1=block,
+                    out=block, in0=ident[:], scalar=neg_root[g][:, a : a + 1], in1=block,
                     op0=ALU.mult, op1=ALU.add,
                 )
 
@@ -183,11 +190,13 @@ def tile_cheblayer_pb_kernel(tc, x, tx1, adj, W, b, out):
         def laplacian(g):
             lap_t = work.tile([P, NODES, PACK], BF16, tag="lap_grp", align_bytes=64)
             for a in range(TILES):
-                nc.vector.tensor_tensor(
+                nc.vector.scalar_tensor_tensor(
                     out=lap_t[:, tile_cols(a), :],
                     in0=rows_turned[g, a][:].rearrange("p t c -> p c t"),
+                    scalar=-1.0,
                     in1=inv[g][:].unsqueeze(1).to_broadcast([P, P, PACK]),
-                    op=ALU.mult,
+                    op0=ALU.mult,
+                    op1=ALU.mult,
                 )
             lap_grp[g] = lap_t
 
@@ -279,6 +288,7 @@ def tile_cheblayer_pb_kernel(tc, x, tx1, adj, W, b, out):
                 x_q[s] = quantise(x_grp[s], "x")
             if live(s + 1):
                 inverse_roots(s + 1)
+                scale_rows_on_scalar(s + 1)
             if live(s):
                 lap_q[s] = quantise(lap_grp[s], "lap")
                 first_product(s)
@@ -299,8 +309,8 @@ def tile_cheblayer_pb_kernel(tc, x, tx1, adj, W, b, out):
                 tx2_grp[s] = work.tile([P, NODES, PACK], BF16, tag="tx2_grp", name="tx2_grp", align_bytes=64)
                 tx2_q[s] = mx_operand("tx2")
             if live(s + 1):
-                scale_rows(s + 1)
-                add_diagonal(s + 1)
+                scale_rows_on_vector(s + 1)
+                subtract_diagonal(s + 1)
             for a in range(TILES):
                 if live(s):
                     second_order(s, a)

from contextlib import ExitStack

import concourse.mybir as mybir
from concourse.masks import make_identity

F32 = mybir.dt.float32
BF16 = mybir.dt.bfloat16
U32 = mybir.dt.uint32
U8 = mybir.dt.uint8
FP8X4 = mybir.dt.float8_e4m3fn_x4
ALU = mybir.AluOpType
ACT = mybir.ActivationFunctionType

P = 128
PACK = 4
GRAPHS = 8
NODES = 512
FEATS = 512
OUTS = 128
ORDERS = 3
TILES = NODES // P
EPS = 1e-6
VECTOR_ROW_TILES = 3

FLOPS = 2 * GRAPHS * (NODES * NODES * FEATS + ORDERS * NODES * FEATS * OUTS)


def tile_cheblayer_pb_kernel(tc, x, tx1, adj, W, b, out):
    nc = tc.nc
    with ExitStack() as ctx:
        const = ctx.enter_context(tc.tile_pool(name="const", bufs=1))
        inputs = ctx.enter_context(tc.tile_pool(name="inputs", bufs=GRAPHS))
        small = ctx.enter_context(tc.tile_pool(name="small", bufs=3))
        work = ctx.enter_context(tc.tile_pool(name="work", bufs=2))
        chain = ctx.enter_context(tc.psum_pool(name="chain", bufs=TILES))
        turned = ctx.enter_context(tc.psum_pool(name="turned", bufs=4))
        ctx.enter_context(tc.manual_schedule())

        x_nat, tx1_nat, adj_nat = {}, {}, {}
        deg, root, neg_root, inv, rows = {}, {}, {}, {}, {}
        x_grp, lap_q, tx1_node_q, x_q, tx1_feat_q, tx2_q = {}, {}, {}, {}, {}, {}
        tx1_feat_grp, tx1_node_grp, lap_grp, tx2_grp = {}, {}, {}, {}
        rows_turned, prod, out_by_feat, out_turned, out_by_node = {}, {}, {}, {}, {}

        eps = const.tile([P, 1], F32)
        nc.vector.memset(eps[:], EPS)
        warm = const.tile([P, 1], F32)
        nc.scalar.activation(out=warm[:], in_=eps[:], func=ACT.Sqrt)
        ident = const.tile([P, P], F32)
        make_identity(nc, ident[:])
        ident_bf = const.tile([P, P], BF16)
        make_identity(nc, ident_bf[:])
        scrap = const.tile([P, TILES, NODES], BF16)

        def load_adjacency(g, pieces):
            adj_t = inputs.tile([P, TILES, NODES], BF16, tag="adj_nat")
            adj_rows = adj[g].rearrange("(a p) j -> p a j", p=P)
            step = TILES // pieces
            for a in range(0, TILES, step):
                nc.sync.dma_start(out=adj_t[:, a : a + step, :], in_=adj_rows[:, a : a + step, :])
            adj_nat[g] = adj_t

        def load_features(g):
            tx1_t = inputs.tile([P, TILES, FEATS], BF16, tag="tx1_nat")
            nc.sync.dma_start(out=tx1_t[:], in_=tx1[g].rearrange("(a p) f -> p a f", p=P))
            x_t = inputs.tile([P, TILES, FEATS], BF16, tag="x_nat")
            nc.sync.dma_start(out=x_t[:], in_=x[g].rearrange("(a p) f -> p a f", p=P))
            tx1_nat[g], x_nat[g] = tx1_t, x_t

        load_adjacency(0, pieces=TILES)
        w_nat = const.tile([P, ORDERS * 2, 2 * OUTS], BF16)
        nc.sync.dma_start(
            out=w_nat[:], in_=W.rearrange("k (u p e) o -> p (k u) (e o)", u=2, e=2)
        )
        b_rows = const.tile([P, P], BF16)
        nc.vector.memset(b_rows[:], 0.0)
        nc.sync.dma_start(out=b_rows[0:ORDERS, :], in_=b)
        load_features(0)
        for g in range(1, GRAPHS):
            load_adjacency(g, pieces=1)
            load_features(g)

        def mx_operand(tag):
            codes = work.tile([P, NODES], U32, tag=tag + "_codes", name=tag + "_codes", align_bytes=64)
            scales = work.tile([P, NODES], U8, tag=tag + "_scales", name=tag + "_scales", align_bytes=64)
            return codes, scales

        def quantise_cols(grouped, operand, cols):
            nc.vector.quantize_mx(
                out=operand[0][:, cols].bitcast(FP8X4),
                scales=operand[1][:, cols],
                in_=grouped[:, cols, :].rearrange("p c t -> p (c t)"),
            )

        def quantise(grouped, tag):
            operand = mx_operand(tag)
            quantise_cols(grouped, operand, slice(0, NODES))
            return operand

        def mx(out_ap, stationary, s_cols, moving, m_cols, start, stop):
            nc.tensor.matmul_mx(
                out=out_ap,
                lhsT=stationary[0][:, s_cols].bitcast(FP8X4),
                lhsT_scale=stationary[1][:, s_cols],
                rhs=moving[0][:, m_cols].bitcast(FP8X4),
                rhs_scale=moving[1][:, m_cols],
                start=start,
                stop=stop,
            )

        def tile_cols(a):
            return slice(a * P, (a + 1) * P)

        def half_cols(h):
            return slice(h * NODES // 2, (h + 1) * NODES // 2)

        w_grp = const.tile([P, ORDERS, OUTS, PACK], BF16, align_bytes=64)
        w_codes = const.tile([P, ORDERS * OUTS], U32, align_bytes=64)
        w_scales = const.tile([P, ORDERS * OUTS], U8, align_bytes=64)
        bias_col = const.tile([P, 1], F32)

        def prepare_weights():
            for k in range(ORDERS):
                nc.vector.tensor_copy(
                    out=w_grp[:, k].rearrange("p o (u e) -> p o u e", u=2),
                    in_=w_nat[:, 2 * k : 2 * k + 2, :].rearrange("p u (e o) -> p o u e", e=2),
                )
            for k in range(ORDERS):
                nc.vector.quantize_mx(
                    out=w_codes[:, tile_cols(k)].bitcast(FP8X4),
                    scales=w_scales[:, tile_cols(k)],
                    in_=w_grp[:, k].rearrange("p o t -> p (o t)"),
                )
            bank = turned.tile([P, P], BF16, tag="turned")
            nc.tensor.transpose(bank[:], b_rows[:], ident_bf[:])
            nc.vector.tensor_reduce(
                out=bias_col[:], in_=bank[:, 0:ORDERS], axis=mybir.AxisListType.X, op=ALU.add
            )

        def degrees(g):
            deg_t = small.tile([P, TILES], F32, tag="deg")
            for a in range(TILES):
                nc.scalar.activation(
                    out=scrap[:, a, :], in_=adj_nat[g][:, a, :], func=ACT.Copy,
                    accum_out=deg_t[:, a : a + 1],
                )
            deg[g] = deg_t

        def roots(g):
            root_t = small.tile([P, TILES], F32, tag="root")
            nc.scalar.activation(out=root_t[:], in_=deg[g][:], func=ACT.Sqrt, bias=eps[:, 0:1])
            neg_t = small.tile([P, TILES], F32, tag="neg_root")
            nc.scalar.activation(out=neg_t[:], in_=root_t[:], func=ACT.Copy, scale=-1.0)
            root[g], neg_root[g] = root_t, neg_t

        def inverse_roots(g):
            inv_t = small.tile([P, TILES], F32, tag="inv")
            nc.vector.reciprocal(out=inv_t[:], in_=root[g][:])
            inv[g] = inv_t

        def scale_rows_on_scalar(g):
            rows[g] = work.tile([P, TILES, NODES], F32, tag="rows", name="rows")
            for a in range(VECTOR_ROW_TILES, TILES):
                nc.scalar.activation(
                    out=rows[g][:, a, :], in_=adj_nat[g][:, a, :], func=ACT.Copy,
                    scale=inv[g][:, a : a + 1],
                )

        def scale_rows_on_vector(g):
            for a in range(VECTOR_ROW_TILES):
                nc.vector.tensor_scalar(
                    out=rows[g][:, a, :], in0=adj_nat[g][:, a, :],
                    scalar1=inv[g][:, a : a + 1], scalar2=None, op0=ALU.mult,
                )

        def subtract_diagonal(g):
            for a in range(TILES):
                block = rows[g][:, a, tile_cols(a)]
                nc.vector.scalar_tensor_tensor(
                    out=block, in0=ident[:], scalar=neg_root[g][:, a : a + 1], in1=block,
                    op0=ALU.mult, op1=ALU.add,
                )

        def turn_rows(g, a):
            bank = chain.tile([P, PACK, P], F32, tag="chain")
            for t in range(PACK):
                nc.tensor.transpose(bank[:, t, :], rows[g][:, a, tile_cols(t)], ident[:])
            rows_turned[g, a] = bank

        def laplacian(g):
            lap_t = work.tile([P, NODES, PACK], BF16, tag="lap_grp", align_bytes=64)
            for a in range(TILES):
                nc.vector.scalar_tensor_tensor(
                    out=lap_t[:, tile_cols(a), :],
                    in0=rows_turned[g, a][:].rearrange("p t c -> p c t"),
                    scalar=-1.0,
                    in1=inv[g][:].unsqueeze(1).to_broadcast([P, P, PACK]),
                    op0=ALU.mult,
                    op1=ALU.mult,
                )
            lap_grp[g] = lap_t

        def group_by_node(g):
            grp = work.tile([P, FEATS, PACK], BF16, tag="tx1_node_grp", align_bytes=64)
            src = tx1_nat[g][:].rearrange("p t (u m e) -> p u m e t", u=2, e=2)
            dst = grp[:].rearrange("p (u e m) t -> p u m e t", u=2, e=2)
            for u in range(2):
                nc.scalar.copy(out=dst[:, u], in_=src[:, u])
            tx1_node_grp[g] = grp

        def turn_features(nat, tag):
            grp = work.tile([P, NODES, PACK], BF16, tag=tag, name=tag, align_bytes=64)
            words_in = nat[:].bitcast(F32)
            words_out = (
                grp[:].rearrange("p i t -> p (i t)").bitcast(F32).rearrange("p (i u) -> p i u", u=2)
            )
            for h in range(2):
                bank = turned.tile([P, 2, 2 * P], F32, tag="turned")
                for u in range(2):
                    for a2 in range(2):
                        nc.tensor.transpose(
                            bank[:, u, tile_cols(a2)], words_in[:, 2 * h + a2, tile_cols(u)], ident[:]
                        )
                nc.scalar.copy(
                    out=words_out[:, 2 * P * h : 2 * P * (h + 1), :],
                    in_=bank[:].rearrange("p u c -> p c u"),
                )
            return grp

        def first_product(g):
            for a in range(TILES):
                bank = chain.tile([P, PACK, P], F32, tag="chain")
                for v in range(PACK):
                    mx(bank[:, v, :], tx1_node_q[g], tile_cols(v), lap_q[g], tile_cols(a), True, True)
                prod[g, a] = bank

        def second_order(g, a):
            nc.vector.scalar_tensor_tensor(
                out=tx2_grp[g][:, tile_cols(a), :],
                in0=prod[g, a][:].rearrange("p v c -> p c v"),
                scalar=2.0,
                in1=x_grp[g][:, tile_cols(a), :],
                op0=ALU.mult,
                op1=ALU.subtract,
            )

        def output_product(g, h):
            if h == 0:
                out_by_feat[g] = work.tile([P, NODES], F32, tag="out_by_feat", name="out_by_feat")
            acc = turned.tile([P, NODES // 2], F32, tag="turned")
            terms = (x_q[g], tx1_feat_q[g], tx2_q[g])
            for k in range(ORDERS):
                mx(acc[:], (w_codes, w_scales), tile_cols(k), terms[k], half_cols(h),
                   k == 0, k == ORDERS - 1)
            nc.scalar.activation(
                out=out_by_feat[g][:, half_cols(h)], in_=acc[:], func=ACT.Relu, bias=bias_col[:, 0:1]
            )

        def turn_output(g, h):
            bank = turned.tile([P, 2, OUTS], F32, tag="turned")
            for a2 in range(2):
                nc.tensor.transpose(bank[:, a2, :], out_by_feat[g][:, tile_cols(2 * h + a2)], ident[:])
            out_turned[g, h] = bank

        def store_output(g, h):
            if h == 0:
                out_by_node[g] = work.tile([P, TILES, OUTS], F32, tag="out_by_node", name="out_by_node")
            tiles = slice(2 * h, 2 * h + 2)
            nc.scalar.copy(out=out_by_node[g][:, tiles, :], in_=out_turned[g, h][:])
            nc.sync.dma_start(
                out=out[g].rearrange("(a p) o -> p a o", p=P)[:, tiles, :], in_=out_by_node[g][:, tiles, :]
            )

        def live(g):
            return 0 <= g < GRAPHS

        for s in range(-2, GRAPHS + 1):
            if s == -1:
                prepare_weights()
            if live(s - 1):
                output_product(s - 1, 0)
                output_product(s - 1, 1)
            if live(s):
                laplacian(s)
            if live(s + 1):
                x_grp[s + 1] = turn_features(x_nat[s + 1], "x_grp")
            if live(s):
                x_q[s] = quantise(x_grp[s], "x")
            if live(s + 1):
                inverse_roots(s + 1)
                scale_rows_on_scalar(s + 1)
            if live(s):
                lap_q[s] = quantise(lap_grp[s], "lap")
                first_product(s)
            if live(s - 1):
                turn_output(s - 1, 0)
                turn_output(s - 1, 1)
            if live(s + 1):
                tx1_feat_grp[s + 1] = turn_features(tx1_nat[s + 1], "tx1_feat_grp")
            if live(s - 1):
                store_output(s - 1, 0)
                store_output(s - 1, 1)
            if live(s + 2):
                degrees(s + 2)
                roots(s + 2)
                group_by_node(s + 2)
            if live(s):
                tx1_feat_q[s] = quantise(tx1_feat_grp[s], "tx1_feat")
                tx2_grp[s] = work.tile([P, NODES, PACK], BF16, tag="tx2_grp", name="tx2_grp", align_bytes=64)
                tx2_q[s] = mx_operand("tx2")
            if live(s + 1):
                scale_rows_on_vector(s + 1)
                subtract_diagonal(s + 1)
            for a in range(TILES):
                if live(s):
                    second_order(s, a)
                if live(s + 1):
                    turn_rows(s + 1, a)
                if live(s) and a == TILES - 2:
                    quantise_cols(tx2_grp[s], tx2_q[s], half_cols(0))
            if live(s + 1):
                tx1_node_q[s + 1] = quantise(tx1_node_grp[s + 1], "tx1_node")
            if live(s):
                quantise_cols(tx2_grp[s], tx2_q[s], half_cols(1))
